import numpy as np
import ml_dtypes


def mxq(x, axis, fmt="e4m3"):
    dtype, down = {"e4m3": (ml_dtypes.float8_e4m3fn, 7), "e5m2": (ml_dtypes.float8_e5m2, 14)}[fmt]
    v = np.moveaxis(np.asarray(x, np.float32).astype(ml_dtypes.bfloat16).astype(np.float64), axis, -1)
    blocks = v.reshape(v.shape[:-1] + (-1, 32))
    amax = np.abs(blocks).max(-1, keepdims=True)
    byte = np.maximum(np.where(amax > 0, np.frexp(amax)[1] - 1 + 127, 0) - down, 1)
    scale = np.exp2(byte - 127.0)
    codes = (blocks / scale).astype(np.float32).astype(dtype).astype(np.float64)
    return np.moveaxis((codes * scale).reshape(v.shape), -1, axis)


WIDE = False


def mx_kscale(k):
    if not WIDE:
        return np.ones(k)
    levels = np.array([10, -10, 5, -5, 0])
    a = np.random.permutation(np.resize(levels, k // 512 * 4)).reshape(k // 512, 4)
    idx = np.arange(k)
    return np.exp2(a[idx // 512, idx % 128 // 32])


BF16 = ml_dtypes.bfloat16


def bf(x):
    return np.asarray(x, np.float32).astype(BF16)


def f64(x):
    return np.asarray(x).astype(np.float64)


B, S, IQ, OQ, Q = 4, 1024, 512, 128, 4


def setup_inputs():
    s = mx_kscale(IQ)
    sw = 0.5 / np.sqrt(IQ)
    return {"x": bf((np.random.standard_normal((B, S, IQ, Q)) * s[:, None]).reshape(B, S, IQ * Q)),
            "wr": bf(np.random.standard_normal((OQ, IQ)) * sw / s),
            "wi": bf(np.random.standard_normal((OQ, IQ)) * sw / s),
            "wj": bf(np.random.standard_normal((OQ, IQ)) * sw / s),
            "wk": bf(np.random.standard_normal((OQ, IQ)) * sw / s),
            "bias": bf(np.random.standard_normal(OQ * Q) * 0.3)}


def reference(x, wr, wi, wj, wk, bias):
    xq = f64(x).reshape(B * S, IQ, Q)
    xr = mxq(xq[:, :, 0], 1, "e4m3")
    xi = mxq(xq[:, :, 1], 1, "e4m3")
    xj = mxq(xq[:, :, 2], 1, "e4m3")
    xk = mxq(xq[:, :, 3], 1, "e4m3")
    qr = mxq(f64(wr), 1, "e4m3")
    qi = mxq(f64(wi), 1, "e4m3")
    qj = mxq(f64(wj), 1, "e4m3")
    qk = mxq(f64(wk), 1, "e4m3")
    Ar = xr @ qr.T
    Br = xi @ qr.T
    Cr = xj @ qr.T
    Dr = xk @ qr.T
    Ai = xr @ qi.T
    Bi = xi @ qi.T
    Aj = xr @ qj.T
    Cj = xj @ qj.T
    Ak = xr @ qk.T
    Dk = xk @ qk.T
    or_ = Ar - Bi - Cj - Dk
    oi_ = Br + Ai + Dk - Cj
    oj_ = Cr - Dk + Aj + Bi
    ok_ = Dr + Cj - Bi + Ak
    out = np.stack([or_, oi_, oj_, ok_], axis=-1).reshape(B, S, Q * OQ)
    return out + f64(bias)[None, None, :]

@@ -1,0 +1,173 @@
+from contextlib import ExitStack
+
+import concourse.masks as masks
+import concourse.mybir as mybir
+
+BF16 = mybir.dt.bfloat16
+F32 = mybir.dt.float32
+U32 = mybir.dt.uint32
+U8 = mybir.dt.uint8
+FP8X4 = mybir.dt.float8_e4m3fn_x4
+
+P = 128
+PACK = 4
+HALVES = 2
+Q = 4
+IQ = 512
+OQ = 128
+ROWS = 4096
+TILES = 2
+CHUNK = TILES * P
+N_CHUNKS = ROWS // CHUNK
+X_BUFS = 4
+AHEAD = 2
+SPLIT = 336
+
+FLOPS = 2 * ROWS * IQ * OQ * 10
+
+TERM = (
+    ((0, 1.0), (1, 1.0), (2, 1.0), (3, 1.0)),
+    ((1, -1.0), (0, 1.0), (1, 1.0), (1, -1.0)),
+    ((2, -1.0), (2, -1.0), (0, 1.0), (2, 1.0)),
+    ((3, -1.0), (3, 1.0), (3, -1.0), (0, 1.0)),
+)
+
+
+def tile_quaternionlinear_pa_t_kernel(tc, x, wr, wi, wj, wk, bias, out):
+    nc = tc.nc
+    x_rows = x.flatten_outer_dims()
+    out_rows = out.flatten_outer_dims()
+
+    with ExitStack() as stack:
+        const = stack.enter_context(tc.tile_pool(name="const", bufs=1))
+        x_pool = stack.enter_context(tc.tile_pool(name="x", bufs=X_BUFS))
+        sorted_pool = stack.enter_context(tc.tile_pool(name="sorted", bufs=AHEAD + 2))
+        grouped_pool = stack.enter_context(tc.tile_pool(name="grouped", bufs=2))
+        mx_pool = stack.enter_context(tc.tile_pool(name="mx", bufs=3))
+        out_pool = stack.enter_context(tc.tile_pool(name="out", bufs=3))
+        bank_pool = stack.enter_context(tc.psum_pool(name="bank", bufs=4))
+        acc_pool = stack.enter_context(tc.psum_pool(name="acc", bufs=4))
+        stack.enter_context(tc.manual_schedule())
+
+        x_raw = {}
+        x_sorted = {}
+        x_codes = {}
+        x_scales = {}
+        sums = {}
+
+        def chunk_rows(dram, j):
+            return dram[j * CHUNK : (j + 1) * CHUNK, :].rearrange("(p t) f -> p t f", t=TILES)
+
+        def load(j):
+            x_raw[j] = x_pool.tile([P, TILES, Q * IQ], BF16, name="x_raw")
+            nc.sync.dma_start(out=x_raw[j][:], in_=chunk_rows(x_rows, j))
+
+        def sort_components(j):
+            x_sorted[j] = sorted_pool.tile([P, TILES, Q, IQ], BF16, name="x_sorted")
+            by_component = x_raw[j][:].rearrange("p t (i c) -> p t c i", c=Q)
+            nc.vector.tensor_copy(
+                out=x_sorted[j][:, :, :, :SPLIT], in_=by_component[:, :, :, :SPLIT]
+            )
+            nc.scalar.copy(out=x_sorted[j][:, :, :, SPLIT:], in_=by_component[:, :, :, SPLIT:])
+            if j + X_BUFS < N_CHUNKS:
+                load(j + X_BUFS)
+
+        def k_on_partitions(planes, grouped):
+            words = planes.bitcast(F32)
+            grouped_words = grouped.bitcast(F32)
+            for first in range(0, Q, 2):
+                bank = bank_pool.tile([P, 2, HALVES, P], F32, name="bank")
+                for c in range(2):
+                    for u in range(HALVES):
+                        nc.tensor.transpose(
+                            bank[:, c, u, :], words[:, first + c, u * P : (u + 1) * P], ident[:]
+                        )
+                nc.scalar.copy(
+                    out=grouped_words[:, first : first + 2],
+                    in_=bank[:].rearrange("p c u r -> p c r u"),
+                )
+
+        def transpose(j):
+            x_grouped[j] = grouped_pool.tile(
+                [P, TILES, Q, P, PACK], BF16, name="x_grouped", align_bytes=64
+            )
+            for t in range(TILES):
+                k_on_partitions(x_sorted[j][:, t], x_grouped[j][:, t])
+
+        def quantise(j):
+            x_codes[j] = mx_pool.tile([P, TILES, Q * P], U32, name="x_codes", align_bytes=64)
+            x_scales[j] = mx_pool.tile([P, TILES, Q * P], U8, name="x_scales", align_bytes=64)
+            nc.vector.quantize_mx(
+                out=x_codes[j][:].rearrange("p t f -> p (t f)").bitcast(FP8X4),
+                scales=x_scales[j][:].rearrange("p t f -> p (t f)"),
+                in_=x_grouped[j][:].rearrange("p t c r k -> p (t c r k)"),
+            )
+
+        def multiply(j):
+            for t in range(TILES):
+                sums[j, t] = acc_pool.tile([P, Q * OQ], F32, name="sums")
+                for a in range(Q):
+                    rows_of_a = slice(a * P, (a + 1) * P)
+                    nc.tensor.matmul_mx(
+                        out=sums[j, t][:],
+                        lhsT=x_codes[j][:, t, rows_of_a].bitcast(FP8X4),
+                        lhsT_scale=x_scales[j][:, t, rows_of_a],
+                        rhs=w_codes[:, a, :].bitcast(FP8X4),
+                        rhs_scale=w_scales[:, a, :],
+                        start=(a == 0),
+                        stop=(a == Q - 1),
+                    )
+
+        def finish(j):
+            result = out_pool.tile([P, TILES, Q * OQ], F32, name="result")
+            for t in range(TILES):
+                nc.vector.tensor_tensor(
+                    out=result[:, t, :].rearrange("p (o c) -> p o c", c=Q),
+                    in0=sums[j, t][:].rearrange("p (c o) -> p o c", c=Q),
+                    in1=bias_all[:].rearrange("p (o c) -> p o c", c=Q),
+                    op=mybir.AluOpType.add,
+                )
+            nc.sync.dma_start(out=chunk_rows(out_rows, j), in_=result[:])
+
+        x_grouped = {}
+
+        w_rows = const.tile([P, Q, IQ], BF16)
+        for m, w in enumerate((wr, wi, wj, wk)):
+            nc.sync.dma_start(out=w_rows[:, m, :], in_=w)
+        for j in range(X_BUFS):
+            load(j)
+        ident = const.tile([P, P], F32)
+        masks.make_identity(nc, ident[:])
+        bias_all = const.tile([P, Q * OQ], BF16)
+        nc.scalar.dma_start(out=bias_all[:], in_=bias.partition_broadcast(P))
+
+        w_grouped = const.tile([P, Q, Q, OQ, PACK], BF16, align_bytes=64)
+        w_codes = const.tile([P, Q, Q * OQ], U32, align_bytes=64)
+        w_scales = const.tile([P, Q, Q * OQ], U8, align_bytes=64)
+        k_on_partitions(w_rows[:], w_grouped[:, 0])
+        sort_components(0)
+        for a in range(1, Q):
+            for c in range(Q):
+                m, sign = TERM[a][c]
+                nc.vector.tensor_scalar_mul(
+                    out=w_grouped[:, a, c], in0=w_grouped[:, 0, m], scalar1=sign
+                )
+        for a in range(Q):
+            nc.vector.quantize_mx(
+                out=w_codes[:, a, :].bitcast(FP8X4),
+                scales=w_scales[:, a, :],
+                in_=w_grouped[:, a].rearrange("p c o t -> p (c o t)"),
+            )
+        sort_components(1)
+
+        for j in range(N_CHUNKS + 1):
+            if j < N_CHUNKS:
+                transpose(j)
+            if j >= 1:
+                multiply(j - 1)
+            if j < N_CHUNKS:
+                quantise(j)
+            if j >= 1:
+                finish(j - 1)
+            if j + AHEAD < N_CHUNKS:
+                sort_components(j + AHEAD)

@@ -21,6 +21,7 @@ CHUNK = TILES * P
 N_CHUNKS = ROWS // CHUNK
 X_BUFS = 4
 AHEAD = 2
+RUN = 4
 SPLIT = 336
 
 FLOPS = 2 * ROWS * IQ * OQ * 10
@@ -64,11 +65,13 @@ def tile_quaternionlinear_pa_t_kernel(tc, x, wr, wi, wj, wk, bias, out):
 
         def sort_components(j):
             x_sorted[j] = sorted_pool.tile([P, TILES, Q, IQ], BF16, name="x_sorted")
-            by_component = x_raw[j][:].rearrange("p t (i c) -> p t c i", c=Q)
-            nc.vector.tensor_copy(
-                out=x_sorted[j][:, :, :, :SPLIT], in_=by_component[:, :, :, :SPLIT]
-            )
-            nc.scalar.copy(out=x_sorted[j][:, :, :, SPLIT:], in_=by_component[:, :, :, SPLIT:])
+            for t in range(TILES):
+                as_loaded = x_raw[j][:, t].rearrange("p (h l c) -> p h c l", l=RUN, c=Q)
+                by_component = x_sorted[j][:, t].rearrange("p c (h l) -> p h c l", l=RUN)
+                nc.vector.tensor_copy(
+                    out=by_component[:, : SPLIT // RUN], in_=as_loaded[:, : SPLIT // RUN]
+                )
+                nc.scalar.copy(out=by_component[:, SPLIT // RUN :], in_=as_loaded[:, SPLIT // RUN :])
             if j + X_BUFS < N_CHUNKS:
                 load(j + X_BUFS)
 

@@ -17,12 +17,11 @@ IQ = 512
 OQ = 128
 ROWS = 4096
 TILES = 2
-CHUNK = TILES * P
-N_CHUNKS = ROWS // CHUNK
+N_CHUNKS = ROWS // (TILES * P)
 X_BUFS = 4
 AHEAD = 2
 RUN = 4
-SPLIT = 336
+SPLIT = 320
 
 FLOPS = 2 * ROWS * IQ * OQ * 10
 
@@ -56,12 +55,14 @@ def tile_quaternionlinear_pa_t_kernel(tc, x, wr, wi, wj, wk, bias, out):
         x_scales = {}
         sums = {}
 
-        def chunk_rows(dram, j):
-            return dram[j * CHUNK : (j + 1) * CHUNK, :].rearrange("(p t) f -> p t f", t=TILES)
+        def tile_rows(dram, j, t):
+            first_row = (j * TILES + t) * P
+            return dram[first_row : first_row + P, :]
 
         def load(j):
             x_raw[j] = x_pool.tile([P, TILES, Q * IQ], BF16, name="x_raw")
-            nc.sync.dma_start(out=x_raw[j][:], in_=chunk_rows(x_rows, j))
+            for t in range(TILES):
+                nc.sync.dma_start(out=x_raw[j][:, t, :], in_=tile_rows(x_rows, j, t))
 
         def sort_components(j):
             x_sorted[j] = sorted_pool.tile([P, TILES, Q, IQ], BF16, name="x_sorted")
@@ -100,11 +101,12 @@ def tile_quaternionlinear_pa_t_kernel(tc, x, wr, wi, wj, wk, bias, out):
         def quantise(j):
             x_codes[j] = mx_pool.tile([P, TILES, Q * P], U32, name="x_codes", align_bytes=64)
             x_scales[j] = mx_pool.tile([P, TILES, Q * P], U8, name="x_scales", align_bytes=64)
-            nc.vector.quantize_mx(
-                out=x_codes[j][:].rearrange("p t f -> p (t f)").bitcast(FP8X4),
-                scales=x_scales[j][:].rearrange("p t f -> p (t f)"),
-                in_=x_grouped[j][:].rearrange("p t c r k -> p (t c r k)"),
-            )
+            for t in range(TILES):
+                nc.vector.quantize_mx(
+                    out=x_codes[j][:, t, :].bitcast(FP8X4),
+                    scales=x_scales[j][:, t, :],
+                    in_=x_grouped[j][:, t].rearrange("p c r k -> p (c r k)"),
+                )
 
         def multiply(j):
             for t in range(TILES):
@@ -130,24 +132,33 @@ def tile_quaternionlinear_pa_t_kernel(tc, x, wr, wi, wj, wk, bias, out):
                     in1=bias_all[:].rearrange("p (o c) -> p o c", c=Q),
                     op=mybir.AluOpType.add,
                 )
-            nc.sync.dma_start(out=chunk_rows(out_rows, j), in_=result[:])
+                nc.sync.dma_start(out=tile_rows(out_rows, j, t), in_=result[:, t, :])
 
         x_grouped = {}
 
         w_rows = const.tile([P, Q, IQ], BF16)
         for m, w in enumerate((wr, wi, wj, wk)):
             nc.sync.dma_start(out=w_rows[:, m, :], in_=w)
+        bias_row = const.tile([P, Q * OQ], BF16)
+        nc.vector.memset(bias_row[:], 0.0)
+        nc.sync.dma_start(out=bias_row[0:1, :], in_=bias.unsqueeze(0))
         for j in range(X_BUFS):
             load(j)
         ident = const.tile([P, P], F32)
         masks.make_identity(nc, ident[:])
-        bias_all = const.tile([P, Q * OQ], BF16)
-        nc.scalar.dma_start(out=bias_all[:], in_=bias.partition_broadcast(P))
+        ones = const.tile([P, P], BF16)
+        nc.vector.memset(ones[:], 1.0)
 
         w_grouped = const.tile([P, Q, Q, OQ, PACK], BF16, align_bytes=64)
         w_codes = const.tile([P, Q, Q * OQ], U32, align_bytes=64)
         w_scales = const.tile([P, Q, Q * OQ], U8, align_bytes=64)
         k_on_partitions(w_rows[:], w_grouped[:, 0])
+
+        bias_spread = acc_pool.tile([P, Q * OQ], F32, name="sums")
+        nc.tensor.matmul(out=bias_spread[:], lhsT=ones[:], rhs=bias_row[:], start=True, stop=True)
+        bias_all = const.tile([P, Q * OQ], F32)
+        nc.scalar.copy(out=bias_all[:], in_=bias_spread[:])
+
         sort_components(0)
         for a in range(1, Q):
             for c in range(Q):

@@ -47,7 +47,6 @@ def tile_quaternionlinear_pa_t_kernel(tc, x, wr, wi, wj, wk, bias, out):
         out_pool = stack.enter_context(tc.tile_pool(name="out", bufs=3))
         bank_pool = stack.enter_context(tc.psum_pool(name="bank", bufs=4))
         acc_pool = stack.enter_context(tc.psum_pool(name="acc", bufs=4))
-        stack.enter_context(tc.manual_schedule())
 
         x_raw = {}
         x_sorted = {}

from contextlib import ExitStack

import concourse.masks as masks
import concourse.mybir as mybir

BF16 = mybir.dt.bfloat16
F32 = mybir.dt.float32
U32 = mybir.dt.uint32
U8 = mybir.dt.uint8
FP8X4 = mybir.dt.float8_e4m3fn_x4

P = 128
PACK = 4
HALVES = 2
Q = 4
IQ = 512
OQ = 128
ROWS = 4096
TILES = 2
N_CHUNKS = ROWS // (TILES * P)
X_BUFS = 4
AHEAD = 2
RUN = 4
SPLIT = 320

FLOPS = 2 * ROWS * IQ * OQ * 10

TERM = (
    ((0, 1.0), (1, 1.0), (2, 1.0), (3, 1.0)),
    ((1, -1.0), (0, 1.0), (1, 1.0), (1, -1.0)),
    ((2, -1.0), (2, -1.0), (0, 1.0), (2, 1.0)),
    ((3, -1.0), (3, 1.0), (3, -1.0), (0, 1.0)),
)


def tile_quaternionlinear_pa_t_kernel(tc, x, wr, wi, wj, wk, bias, out):
    nc = tc.nc
    x_rows = x.flatten_outer_dims()
    out_rows = out.flatten_outer_dims()

    with ExitStack() as stack:
        const = stack.enter_context(tc.tile_pool(name="const", bufs=1))
        x_pool = stack.enter_context(tc.tile_pool(name="x", bufs=X_BUFS))
        sorted_pool = stack.enter_context(tc.tile_pool(name="sorted", bufs=AHEAD + 2))
        grouped_pool = stack.enter_context(tc.tile_pool(name="grouped", bufs=2))
        mx_pool = stack.enter_context(tc.tile_pool(name="mx", bufs=3))
        out_pool = stack.enter_context(tc.tile_pool(name="out", bufs=3))
        bank_pool = stack.enter_context(tc.psum_pool(name="bank", bufs=4))
        acc_pool = stack.enter_context(tc.psum_pool(name="acc", bufs=4))

        x_raw = {}
        x_sorted = {}
        x_codes = {}
        x_scales = {}
        sums = {}

        def tile_rows(dram, j, t):
            first_row = (j * TILES + t) * P
            return dram[first_row : first_row + P, :]

        def load(j):
            x_raw[j] = x_pool.tile([P, TILES, Q * IQ], BF16, name="x_raw")
            for t in range(TILES):
                nc.sync.dma_start(out=x_raw[j][:, t, :], in_=tile_rows(x_rows, j, t))

        def sort_components(j):
            x_sorted[j] = sorted_pool.tile([P, TILES, Q, IQ], BF16, name="x_sorted")
            for t in range(TILES):
                as_loaded = x_raw[j][:, t].rearrange("p (h l c) -> p h c l", l=RUN, c=Q)
                by_component = x_sorted[j][:, t].rearrange("p c (h l) -> p h c l", l=RUN)
                nc.vector.tensor_copy(
                    out=by_component[:, : SPLIT // RUN], in_=as_loaded[:, : SPLIT // RUN]
                )
                nc.scalar.copy(out=by_component[:, SPLIT // RUN :], in_=as_loaded[:, SPLIT // RUN :])
            if j + X_BUFS < N_CHUNKS:
                load(j + X_BUFS)

        def k_on_partitions(planes, grouped):
            words = planes.bitcast(F32)
            grouped_words = grouped.bitcast(F32)
            for first in range(0, Q, 2):
                bank = bank_pool.tile([P, 2, HALVES, P], F32, name="bank")
                for c in range(2):
                    for u in range(HALVES):
                        nc.tensor.transpose(
                            bank[:, c, u, :], words[:, first + c, u * P : (u + 1) * P], ident[:]
                        )
                nc.scalar.copy(
                    out=grouped_words[:, first : first + 2],
                    in_=bank[:].rearrange("p c u r -> p c r u"),
                )

        def transpose(j):
            x_grouped[j] = grouped_pool.tile(
                [P, TILES, Q, P, PACK], BF16, name="x_grouped", align_bytes=64
            )
            for t in range(TILES):
                k_on_partitions(x_sorted[j][:, t], x_grouped[j][:, t])

        def quantise(j):
            x_codes[j] = mx_pool.tile([P, TILES, Q * P], U32, name="x_codes", align_bytes=64)
            x_scales[j] = mx_pool.tile([P, TILES, Q * P], U8, name="x_scales", align_bytes=64)
            for t in range(TILES):
                nc.vector.quantize_mx(
                    out=x_codes[j][:, t, :].bitcast(FP8X4),
                    scales=x_scales[j][:, t, :],
                    in_=x_grouped[j][:, t].rearrange("p c r k -> p (c r k)"),
                )

        def multiply(j):
            for t in range(TILES):
                sums[j, t] = acc_pool.tile([P, Q * OQ], F32, name="sums")
                for a in range(Q):
                    rows_of_a = slice(a * P, (a + 1) * P)
                    nc.tensor.matmul_mx(
                        out=sums[j, t][:],
                        lhsT=x_codes[j][:, t, rows_of_a].bitcast(FP8X4),
                        lhsT_scale=x_scales[j][:, t, rows_of_a],
                        rhs=w_codes[:, a, :].bitcast(FP8X4),
                        rhs_scale=w_scales[:, a, :],
                        start=(a == 0),
                        stop=(a == Q - 1),
                    )

        def finish(j):
            result = out_pool.tile([P, TILES, Q * OQ], F32, name="result")
            for t in range(TILES):
                nc.vector.tensor_tensor(
                    out=result[:, t, :].rearrange("p (o c) -> p o c", c=Q),
                    in0=sums[j, t][:].rearrange("p (c o) -> p o c", c=Q),
                    in1=bias_all[:].rearrange("p (o c) -> p o c", c=Q),
                    op=mybir.AluOpType.add,
                )
                nc.sync.dma_start(out=tile_rows(out_rows, j, t), in_=result[:, t, :])

        x_grouped = {}

        w_rows = const.tile([P, Q, IQ], BF16)
        for m, w in enumerate((wr, wi, wj, wk)):
            nc.sync.dma_start(out=w_rows[:, m, :], in_=w)
        bias_row = const.tile([P, Q * OQ], BF16)
        nc.vector.memset(bias_row[:], 0.0)
        nc.sync.dma_start(out=bias_row[0:1, :], in_=bias.unsqueeze(0))
        for j in range(X_BUFS):
            load(j)
        ident = const.tile([P, P], F32)
        masks.make_identity(nc, ident[:])
        ones = const.tile([P, P], BF16)
        nc.vector.memset(ones[:], 1.0)

        w_grouped = const.tile([P, Q, Q, OQ, PACK], BF16, align_bytes=64)
        w_codes = const.tile([P, Q, Q * OQ], U32, align_bytes=64)
        w_scales = const.tile([P, Q, Q * OQ], U8, align_bytes=64)
        k_on_partitions(w_rows[:], w_grouped[:, 0])

        bias_spread = acc_pool.tile([P, Q * OQ], F32, name="sums")
        nc.tensor.matmul(out=bias_spread[:], lhsT=ones[:], rhs=bias_row[:], start=True, stop=True)
        bias_all = const.tile([P, Q * OQ], F32)
        nc.scalar.copy(out=bias_all[:], in_=bias_spread[:])

        sort_components(0)
        for a in range(1, Q):
            for c in range(Q):
                m, sign = TERM[a][c]
                nc.vector.tensor_scalar_mul(
                    out=w_grouped[:, a, c], in0=w_grouped[:, 0, m], scalar1=sign
                )
        for a in range(Q):
            nc.vector.quantize_mx(
                out=w_codes[:, a, :].bitcast(FP8X4),
                scales=w_scales[:, a, :],
                in_=w_grouped[:, a].rearrange("p c o t -> p (c o t)"),
            )
        sort_components(1)

        for j in range(N_CHUNKS + 1):
            if j < N_CHUNKS:
                transpose(j)
            if j >= 1:
                multiply(j - 1)
            if j < N_CHUNKS:
                quantise(j)
            if j >= 1:
                finish(j - 1)
            if j + AHEAD < N_CHUNKS:
                sort_components(j + AHEAD)
